import numpy as np
import ml_dtypes


def mxq(x, axis, fmt="e4m3"):
    dtype, down = {"e4m3": (ml_dtypes.float8_e4m3fn, 7), "e5m2": (ml_dtypes.float8_e5m2, 14)}[fmt]
    v = np.moveaxis(np.asarray(x, np.float32).astype(ml_dtypes.bfloat16).astype(np.float64), axis, -1)
    blocks = v.reshape(v.shape[:-1] + (-1, 32))
    amax = np.abs(blocks).max(-1, keepdims=True)
    byte = np.maximum(np.where(amax > 0, np.frexp(amax)[1] - 1 + 127, 0) - down, 1)
    scale = np.exp2(byte - 127.0)
    codes = (blocks / scale).astype(np.float32).astype(dtype).astype(np.float64)
    return np.moveaxis((codes * scale).reshape(v.shape), -1, axis)


WIDE = False


def mx_kscale(k):
    if not WIDE:
        return np.ones(k)
    levels = np.array([10, -10, 5, -5, 0])
    a = np.random.permutation(np.resize(levels, k // 512 * 4)).reshape(k // 512, 4)
    idx = np.arange(k)
    return np.exp2(a[idx // 512, idx % 128 // 32])


BF16 = ml_dtypes.bfloat16


def bf(x):
    return np.asarray(x, np.float32).astype(BF16)


def f64(x):
    return np.asarray(x).astype(np.float64)


B, T, C, NH, HS, NLQ, NLKV, DHR = 1, 128, 1024, 8, 128, 512, 128, 128
THETA = 10000.0


def rope(v, cos, sin):
    vr = v.reshape(v.shape[:-1] + (-1, 2))
    re, im = vr[..., 0], vr[..., 1]
    c = cos[None, :, None, :]
    s = sin[None, :, None, :]
    return np.stack([re * c - im * s, re * s + im * c], axis=-1).reshape(v.shape)


def setup_inputs():
    s, t = mx_kscale(C), mx_kscale(NLQ)
    ang = np.outer(np.arange(T), 1.0 / THETA ** (np.arange(0, DHR, 2) / DHR))
    return {"x": bf(np.random.standard_normal((B, T, C)) * s),
            "cos": bf(np.cos(ang)),
            "sin": bf(np.sin(ang)),
            "W_dq": bf(np.random.standard_normal((NLQ, C)) / np.sqrt(C) / s[None, :] * t[:, None]),
            "W_uq": bf((np.random.standard_normal((NLQ, C)) / np.sqrt(NLQ) / t[:, None]).reshape(C, NLQ)),
            "W_uk": bf(np.random.standard_normal((C, NLKV)) / np.sqrt(HS)),
            "W_qr": bf(np.random.standard_normal((NH * DHR, NLQ)) / np.sqrt(NLQ) / t[None, :])}


def reference(x, cos, sin, W_dq, W_uq, W_uk, W_qr):
    cq = mxq(mxq(f64(x), 2, "e4m3") @ mxq(f64(W_dq), 1, "e4m3").T, 2, "e4m3")
    k_eff = f64(W_uq).reshape(NLQ, NH, HS).transpose(1, 0, 2) @ f64(W_uk).reshape(NH, HS, NLKV)
    q_abs = cq[:, None] @ mxq(k_eff, 1, "e4m3")[None]
    c_qr = (cq @ mxq(f64(W_qr), 1, "e4m3").T).reshape(B, T, NH, DHR)
    return q_abs, rope(c_qr, f64(cos), f64(sin))

@@ -1,0 +1,248 @@
+from contextlib import ExitStack
+
+import concourse.mybir as mybir
+from concourse.masks import make_identity
+
+F32 = mybir.dt.float32
+BF16 = mybir.dt.bfloat16
+U32 = mybir.dt.uint32
+U8 = mybir.dt.uint8
+FP8X4 = mybir.dt.float8_e4m3fn_x4
+MULT = mybir.AluOpType.mult
+ADD = mybir.AluOpType.add
+
+P = 128
+PACK = 4
+BANK = 512
+C = 1024
+L = 512
+HEADS = 8
+HALF = 64
+
+FLOPS = 2 * P * C * L + 2 * HEADS * L * P * P + 2 * HEADS * P * L * P + 2 * P * L * HEADS * P
+
+
+def tile_causalselfattention_pa_s_kernel(tc, x, cos, sin, W_dq, W_uq, W_uk, W_qr, out_0, out_1):
+    nc = tc.nc
+    with ExitStack() as ctx:
+        keep = ctx.enter_context(tc.tile_pool(name="keep", bufs=1))
+        psum = ctx.enter_context(tc.psum_pool(name="psum", bufs=8))
+        ctx.enter_context(tc.manual_schedule())
+
+        a_sb = keep.tile([P, 2, 2, C], BF16)
+        a_dram = W_uq.rearrange("(v q e two) c -> q v e (two c)", v=2, e=2, two=2)
+        u_sb = keep.tile([P, HEADS, P], BF16)
+        x_sb = keep.tile([P, C], BF16)
+        wdq_sb = keep.tile([P, 2, 2, C], BF16)
+        wdq_dram = W_dq.rearrange("(v q e) c -> q v (e c)", v=2, e=2)
+        wqr_sb = keep.tile([P, 4, 2, L], BF16)
+        wqr_dram = W_qr.rearrange("(b q e) l -> q b (e l)", b=4, e=2)
+        cos_sb = keep.tile([P, HALF], BF16)
+        sin_sb = keep.tile([P, HALF], BF16)
+
+        half_heads = C // 2
+        for first in (0, half_heads):
+            for v in range(2):
+                nc.sync.dma_start(
+                    out=a_sb[:, v, :, first : first + half_heads],
+                    in_=a_dram[:, v, :, first : first + half_heads],
+                )
+            if first == 0:
+                nc.sync.dma_start(out=u_sb[:], in_=W_uk.rearrange("(h d) n -> d h n", h=HEADS))
+        nc.sync.dma_start(out=x_sb[:], in_=x[0])
+        for v in range(2):
+            nc.sync.dma_start(out=wdq_sb[:, v].rearrange("q e c -> q (e c)"), in_=wdq_dram[:, v])
+        for j in range(2):
+            nc.sync.dma_start(
+                out=wqr_sb[:, 2 * j : 2 * j + 2].rearrange("q b e l -> q b (e l)"),
+                in_=wqr_dram[:, 2 * j : 2 * j + 2],
+            )
+        nc.scalar.dma_start(out=cos_sb[:], in_=cos)
+        nc.scalar.dma_start(out=sin_sb[:], in_=sin)
+
+        ident_bf16 = keep.tile([P, P], BF16)
+        make_identity(nc, ident_bf16[:])
+        ident_f32 = keep.tile([P, P], F32)
+        make_identity(nc, ident_f32[:])
+        minus_sin = keep.tile([P, HALF], BF16)
+        nc.gpsimd.tensor_scalar_mul(minus_sin[:], sin_sb[:], -1.0)
+
+        at_sb = keep.tile([P, HEADS, PACK, P], BF16)
+        keff_grouped = keep.tile([P, HEADS * P * PACK], BF16, align_bytes=64)
+        keff_codes = keep.tile([P, HEADS * P], U32, align_bytes=64)
+        keff_scales = keep.tile([P, HEADS * P], U8, align_bytes=64)
+        x_grouped = keep.tile([P, 2 * P * PACK], BF16, align_bytes=64)
+        x_codes = keep.tile([P, 2 * P], U32, align_bytes=64)
+        x_scales = keep.tile([P, 2 * P], U8, align_bytes=64)
+        wdq_grouped = keep.tile([P, PACK * 2 * P * PACK], BF16, align_bytes=64)
+        wdq_codes = keep.tile([P, PACK * 2 * P], U32, align_bytes=64)
+        wdq_scales = keep.tile([P, PACK * 2 * P], U8, align_bytes=64)
+        cq_grouped = keep.tile([P, P * PACK], BF16, align_bytes=64)
+        cq_codes = keep.tile([P, P], U32, align_bytes=64)
+        cq_scales = keep.tile([P, P], U8, align_bytes=64)
+        wqr_grouped = keep.tile([P, HEADS * P * PACK], BF16, align_bytes=64)
+        wqr_codes = keep.tile([P, HEADS * P], U32, align_bytes=64)
+        wqr_scales = keep.tile([P, HEADS * P], U8, align_bytes=64)
+
+        def quantise(codes, scales, grouped, first_word, words):
+            nc.vector.quantize_mx(
+                out=codes[:, first_word : first_word + words].bitcast(FP8X4),
+                scales=scales[:, first_word : first_word + words],
+                in_=grouped[:, PACK * first_word : PACK * (first_word + words)],
+            )
+
+        def transpose_words(rows, grouped_words):
+            words = rows.bitcast(F32)
+            bank = psum.tile([P, BANK], F32, tag="bank")
+            for piece in range(BANK // P):
+                nc.tensor.transpose(
+                    bank[:, P * piece : P * (piece + 1)], words[:, P * piece : P * (piece + 1)], ident_f32[:]
+                )
+            nc.scalar.copy(
+                out=grouped_words.rearrange("q (g r v) -> q g r v", r=P, v=2),
+                in_=bank[:].rearrange("q (g v r) -> q g r v", r=P, v=2),
+            )
+
+        def transpose_a(pair):
+            bank = psum.tile([P, 2 * PACK * P], BF16, tag="bank")
+            for piece in range(2 * PACK):
+                h, t = 2 * pair + piece // PACK, piece % PACK
+                nc.tensor.transpose(
+                    bank[:, P * piece : P * (piece + 1)], a_sb[:, t // 2, t % 2, P * h : P * (h + 1)], ident_bf16[:]
+                )
+            nc.scalar.copy(out=at_sb[:, 2 * pair : 2 * pair + 2].rearrange("d h t q -> d (h t q)"), in_=bank[:])
+
+        def multiply_keff(pair):
+            for h in (2 * pair, 2 * pair + 1):
+                bank = psum.tile([P, BANK], F32, tag="bank")
+                for t in range(PACK):
+                    nc.tensor.matmul(
+                        out=bank[:, P * t : P * (t + 1)], lhsT=at_sb[:, h, t, :], rhs=u_sb[:, h, :], start=True, stop=True
+                    )
+                grouped = keff_grouped[:, BANK * h : BANK * (h + 1)].rearrange("q (n t) -> q n t", t=PACK)
+                by_column = bank[:].rearrange("q (t n) -> q n t", t=PACK)
+                if h % 2 == 0:
+                    nc.scalar.copy(out=grouped, in_=by_column)
+                else:
+                    nc.vector.tensor_copy(out=grouped, in_=by_column)
+
+        pairs = HEADS // 2
+        transpose_a(0)
+        transpose_a(1)
+        for pair in range(pairs):
+            multiply_keff(pair)
+            if pair + 2 < pairs:
+                transpose_a(pair + 2)
+            if pair >= 1:
+                quantise(keff_codes, keff_scales, keff_grouped, 2 * P * (pair - 1), 2 * P)
+
+        transpose_words(x_sb[:], x_grouped[:].bitcast(F32))
+        quantise(keff_codes, keff_scales, keff_grouped, 2 * P * (pairs - 1), 2 * P)
+        for s in range(PACK):
+            transpose_words(
+                wdq_sb[:, s // 2, s % 2, :], wdq_grouped[:, 2 * BANK * s : 2 * BANK * (s + 1)].bitcast(F32)
+            )
+            if s == 0:
+                quantise(x_codes, x_scales, x_grouped, 0, 2 * P)
+            else:
+                quantise(wdq_codes, wdq_scales, wdq_grouped, 2 * P * (s - 1), 2 * P)
+
+        def transpose_wqr(b):
+            bank = psum.tile([P, BANK], F32, tag="bank")
+            for piece in range(BANK // P):
+                e, v = piece // 2, piece % 2
+                nc.tensor.transpose(
+                    bank[:, P * piece : P * (piece + 1)],
+                    wqr_sb[:, b, e, :].bitcast(F32)[:, P * v : P * (v + 1)],
+                    ident_f32[:],
+                )
+            grouped_words = wqr_grouped[:].bitcast(F32).rearrange("q (j e b r v) -> q j e b r v", j=2, e=2, b=2, v=2)
+            nc.scalar.copy(
+                out=grouped_words[:, b // 2, :, b % 2, :, :], in_=bank[:].rearrange("q (e v r) -> q e r v", e=2, v=2)
+            )
+
+        transpose_wqr(0)
+        quantise(wdq_codes, wdq_scales, wdq_grouped, 2 * P * (PACK - 1), 2 * P)
+        transpose_wqr(1)
+
+        cq_bank = psum.tile([P, BANK], F32, tag="bank")
+        for s in range(PACK):
+            for g in range(2):
+                stationary = slice(2 * P * s + P * g, 2 * P * s + P * (g + 1))
+                moving = slice(P * g, P * (g + 1))
+                nc.tensor.matmul_mx(
+                    out=cq_bank[:, P * s : P * (s + 1)],
+                    lhsT=wdq_codes[:, stationary].bitcast(FP8X4),
+                    lhsT_scale=wdq_scales[:, stationary],
+                    rhs=x_codes[:, moving].bitcast(FP8X4),
+                    rhs_scale=x_scales[:, moving],
+                    start=(g == 0),
+                    stop=(g == 1),
+                )
+        nc.vector.tensor_copy(
+            out=cq_grouped[:].rearrange("q (r t) -> q r t", t=PACK), in_=cq_bank[:].rearrange("q (t r) -> q r t", t=PACK)
+        )
+        transpose_wqr(2)
+        quantise(wqr_codes, wqr_scales, wqr_grouped, 0, BANK)
+        quantise(cq_codes, cq_scales, cq_grouped, 0, P)
+        transpose_wqr(3)
+        quantise(wqr_codes, wqr_scales, wqr_grouped, BANK, BANK)
+
+        def times_cq(codes, scales, j):
+            bank = psum.tile([P, BANK], F32, tag="bank")
+            columns = slice(BANK * j, BANK * (j + 1))
+            nc.tensor.matmul_mx(
+                out=bank[:],
+                lhsT=cq_codes[:].bitcast(FP8X4),
+                lhsT_scale=cq_scales[:],
+                rhs=codes[:, columns].bitcast(FP8X4),
+                rhs_scale=scales[:, columns],
+                start=True,
+                stop=True,
+            )
+            return bank
+
+        def absorbed(j):
+            bank = times_cq(keff_codes, keff_scales, j)
+            q_abs = keep.tile([P, BANK], F32, name="q_abs%d" % j)
+            nc.scalar.copy(out=q_abs[:], in_=bank[:])
+            nc.sync.dma_start(
+                out=out_0[0, 4 * j : 4 * j + 4].rearrange("h r n -> r h n"), in_=q_abs[:].rearrange("r (h n) -> r h n", n=P)
+            )
+
+        def rotated(j):
+            bank = times_cq(wqr_codes, wqr_scales, j)
+            half = BANK // 2
+            by_cos = keep.tile([P, BANK], F32, name="by_cos%d" % j)
+            by_sin = keep.tile([P, BANK], F32, name="by_sin%d" % j)
+            q_r = keep.tile([P, BANK], F32, name="q_r%d" % j)
+            nc.vector.tensor_tensor(
+                out=by_cos[:].rearrange("r (k i) -> r k i", i=HALF),
+                in0=bank[:].rearrange("r (k i) -> r k i", i=HALF),
+                in1=cos_sb[:].unsqueeze(1).to_broadcast([P, BANK // HALF, HALF]),
+                op=MULT,
+            )
+            nc.vector.tensor_tensor(
+                out=by_sin[:, 0:half].rearrange("r (k i) -> r k i", i=HALF),
+                in0=bank[:, half:BANK].rearrange("r (k i) -> r k i", i=HALF),
+                in1=minus_sin[:].unsqueeze(1).to_broadcast([P, half // HALF, HALF]),
+                op=MULT,
+            )
+            nc.vector.tensor_tensor(
+                out=by_sin[:, half:BANK].rearrange("r (k i) -> r k i", i=HALF),
+                in0=bank[:, 0:half].rearrange("r (k i) -> r k i", i=HALF),
+                in1=sin_sb[:].unsqueeze(1).to_broadcast([P, half // HALF, HALF]),
+                op=MULT,
+            )
+            nc.vector.tensor_tensor(
+                out=q_r[:].rearrange("r (c e) -> r c e", e=2),
+                in0=by_cos[:].rearrange("r (e c) -> r c e", e=2),
+                in1=by_sin[:].rearrange("r (e c) -> r c e", e=2),
+                op=ADD,
+            )
+            nc.sync.dma_start(out=out_1[0, :, 4 * j : 4 * j + 4, :].rearrange("r h d -> r (h d)"), in_=q_r[:])
+
+        rotated(0)
+        absorbed(0)
+        absorbed(1)
+        rotated(1)

@@ -40,30 +40,32 @@ def tile_causalselfattention_pa_s_kernel(tc, x, cos, sin, W_dq, W_uq, W_uk, W_qr
         cos_sb = keep.tile([P, HALF], BF16)
         sin_sb = keep.tile([P, HALF], BF16)
 
-        half_heads = C // 2
-        for first in (0, half_heads):
+        def load_a(first_head):
+            columns = slice(P * first_head, P * (first_head + 4))
             for v in range(2):
-                nc.sync.dma_start(
-                    out=a_sb[:, v, :, first : first + half_heads],
-                    in_=a_dram[:, v, :, first : first + half_heads],
-                )
-            if first == 0:
-                nc.sync.dma_start(out=u_sb[:], in_=W_uk.rearrange("(h d) n -> d h n", h=HEADS))
-        nc.sync.dma_start(out=x_sb[:], in_=x[0])
-        for v in range(2):
-            nc.sync.dma_start(out=wdq_sb[:, v].rearrange("q e c -> q (e c)"), in_=wdq_dram[:, v])
-        for j in range(2):
+                nc.sync.dma_start(out=a_sb[:, v, :, columns], in_=a_dram[:, v, :, columns])
+
+        def load_wqr(j):
             nc.sync.dma_start(
                 out=wqr_sb[:, 2 * j : 2 * j + 2].rearrange("q b e l -> q b (e l)"),
                 in_=wqr_dram[:, 2 * j : 2 * j + 2],
             )
+
+        nc.sync.dma_start(out=x_sb[:], in_=x[0])
+        load_a(0)
+        for v in range(2):
+            nc.sync.dma_start(out=wdq_sb[:, v].rearrange("q e c -> q (e c)"), in_=wdq_dram[:, v])
+        nc.sync.dma_start(out=u_sb[:], in_=W_uk.rearrange("(h d) n -> d h n", h=HEADS))
+        load_wqr(0)
+        load_a(4)
+        load_wqr(1)
         nc.scalar.dma_start(out=cos_sb[:], in_=cos)
         nc.scalar.dma_start(out=sin_sb[:], in_=sin)
 
-        ident_bf16 = keep.tile([P, P], BF16)
-        make_identity(nc, ident_bf16[:])
         ident_f32 = keep.tile([P, P], F32)
         make_identity(nc, ident_f32[:])
+        ident_bf16 = keep.tile([P, P], BF16)
+        make_identity(nc, ident_bf16[:])
         minus_sin = keep.tile([P, HALF], BF16)
         nc.gpsimd.tensor_scalar_mul(minus_sin[:], sin_sb[:], -1.0)
 
@@ -91,61 +93,29 @@ def tile_causalselfattention_pa_s_kernel(tc, x, cos, sin, W_dq, W_uq, W_uk, W_qr
                 in_=grouped[:, PACK * first_word : PACK * (first_word + words)],
             )
 
-        def transpose_words(rows, grouped_words):
+        def empty(number, out, in_):
+            if number % 2 == 0:
+                nc.vector.tensor_copy(out=out, in_=in_)
+            else:
+                nc.scalar.copy(out=out, in_=in_)
+
+        SCALAR = 1
+
+        def transpose_words(number, rows, grouped_words):
             words = rows.bitcast(F32)
             bank = psum.tile([P, BANK], F32, tag="bank")
             for piece in range(BANK // P):
                 nc.tensor.transpose(
                     bank[:, P * piece : P * (piece + 1)], words[:, P * piece : P * (piece + 1)], ident_f32[:]
                 )
-            nc.scalar.copy(
+            empty(
+                number,
                 out=grouped_words.rearrange("q (g r v) -> q g r v", r=P, v=2),
                 in_=bank[:].rearrange("q (g v r) -> q g r v", r=P, v=2),
             )
 
-        def transpose_a(pair):
-            bank = psum.tile([P, 2 * PACK * P], BF16, tag="bank")
-            for piece in range(2 * PACK):
-                h, t = 2 * pair + piece // PACK, piece % PACK
-                nc.tensor.transpose(
-                    bank[:, P * piece : P * (piece + 1)], a_sb[:, t // 2, t % 2, P * h : P * (h + 1)], ident_bf16[:]
-                )
-            nc.scalar.copy(out=at_sb[:, 2 * pair : 2 * pair + 2].rearrange("d h t q -> d (h t q)"), in_=bank[:])
-
-        def multiply_keff(pair):
-            for h in (2 * pair, 2 * pair + 1):
-                bank = psum.tile([P, BANK], F32, tag="bank")
-                for t in range(PACK):
-                    nc.tensor.matmul(
-                        out=bank[:, P * t : P * (t + 1)], lhsT=at_sb[:, h, t, :], rhs=u_sb[:, h, :], start=True, stop=True
-                    )
-                grouped = keff_grouped[:, BANK * h : BANK * (h + 1)].rearrange("q (n t) -> q n t", t=PACK)
-                by_column = bank[:].rearrange("q (t n) -> q n t", t=PACK)
-                if h % 2 == 0:
-                    nc.scalar.copy(out=grouped, in_=by_column)
-                else:
-                    nc.vector.tensor_copy(out=grouped, in_=by_column)
-
-        pairs = HEADS // 2
-        transpose_a(0)
-        transpose_a(1)
-        for pair in range(pairs):
-            multiply_keff(pair)
-            if pair + 2 < pairs:
-                transpose_a(pair + 2)
-            if pair >= 1:
-                quantise(keff_codes, keff_scales, keff_grouped, 2 * P * (pair - 1), 2 * P)
-
-        transpose_words(x_sb[:], x_grouped[:].bitcast(F32))
-        quantise(keff_codes, keff_scales, keff_grouped, 2 * P * (pairs - 1), 2 * P)
-        for s in range(PACK):
-            transpose_words(
-                wdq_sb[:, s // 2, s % 2, :], wdq_grouped[:, 2 * BANK * s : 2 * BANK * (s + 1)].bitcast(F32)
-            )
-            if s == 0:
-                quantise(x_codes, x_scales, x_grouped, 0, 2 * P)
-            else:
-                quantise(wdq_codes, wdq_scales, wdq_grouped, 2 * P * (s - 1), 2 * P)
+        def transpose_wdq(s):
+            transpose_words(s, wdq_sb[:, s // 2, s % 2, :], wdq_grouped[:, 2 * BANK * s : 2 * BANK * (s + 1)].bitcast(F32))
 
         def transpose_wqr(b):
             bank = psum.tile([P, BANK], F32, tag="bank")
@@ -157,36 +127,50 @@ def tile_causalselfattention_pa_s_kernel(tc, x, cos, sin, W_dq, W_uq, W_uk, W_qr
                     ident_f32[:],
                 )
             grouped_words = wqr_grouped[:].bitcast(F32).rearrange("q (j e b r v) -> q j e b r v", j=2, e=2, b=2, v=2)
-            nc.scalar.copy(
-                out=grouped_words[:, b // 2, :, b % 2, :, :], in_=bank[:].rearrange("q (e v r) -> q e r v", e=2, v=2)
+            empty(b, out=grouped_words[:, b // 2, :, b % 2, :, :], in_=bank[:].rearrange("q (e v r) -> q e r v", e=2, v=2))
+
+        def transpose_a(pair, number):
+            bank = psum.tile([P, 2 * PACK * P], BF16, tag="bank")
+            for piece in range(2 * PACK):
+                h, t = 2 * pair + piece // PACK, piece % PACK
+                nc.tensor.transpose(
+                    bank[:, P * piece : P * (piece + 1)], a_sb[:, t // 2, t % 2, P * h : P * (h + 1)], ident_bf16[:]
+                )
+            empty(number, out=at_sb[:, 2 * pair : 2 * pair + 2].rearrange("d h t q -> d (h t q)"), in_=bank[:])
+
+        def multiply_keff(h, number):
+            bank = psum.tile([P, BANK], F32, tag="bank")
+            for t in range(PACK):
+                nc.tensor.matmul(
+                    out=bank[:, P * t : P * (t + 1)], lhsT=at_sb[:, h, t, :], rhs=u_sb[:, h, :], start=True, stop=True
+                )
+            empty(
+                number,
+                out=keff_grouped[:, BANK * h : BANK * (h + 1)].rearrange("q (n t) -> q n t", t=PACK),
+                in_=bank[:].rearrange("q (t n) -> q n t", t=PACK),
             )
 
-        transpose_wqr(0)
-        quantise(wdq_codes, wdq_scales, wdq_grouped, 2 * P * (PACK - 1), 2 * P)
-        transpose_wqr(1)
+        def quantise_keff(pair):
+            quantise(keff_codes, keff_scales, keff_grouped, 2 * P * pair, 2 * P)
 
-        cq_bank = psum.tile([P, BANK], F32, tag="bank")
-        for s in range(PACK):
-            for g in range(2):
-                stationary = slice(2 * P * s + P * g, 2 * P * s + P * (g + 1))
-                moving = slice(P * g, P * (g + 1))
-                nc.tensor.matmul_mx(
-                    out=cq_bank[:, P * s : P * (s + 1)],
-                    lhsT=wdq_codes[:, stationary].bitcast(FP8X4),
-                    lhsT_scale=wdq_scales[:, stationary],
-                    rhs=x_codes[:, moving].bitcast(FP8X4),
-                    rhs_scale=x_scales[:, moving],
-                    start=(g == 0),
-                    stop=(g == 1),
-                )
-        nc.vector.tensor_copy(
-            out=cq_grouped[:].rearrange("q (r t) -> q r t", t=PACK), in_=cq_bank[:].rearrange("q (t r) -> q r t", t=PACK)
-        )
-        transpose_wqr(2)
-        quantise(wqr_codes, wqr_scales, wqr_grouped, 0, BANK)
-        quantise(cq_codes, cq_scales, cq_grouped, 0, P)
-        transpose_wqr(3)
-        quantise(wqr_codes, wqr_scales, wqr_grouped, BANK, BANK)
+        def latent():
+            bank = psum.tile([P, BANK], F32, tag="bank")
+            for s in range(PACK):
+                for g in range(2):
+                    stationary = slice(2 * P * s + P * g, 2 * P * s + P * (g + 1))
+                    moving = slice(P * g, P * (g + 1))
+                    nc.tensor.matmul_mx(
+                        out=bank[:, P * s : P * (s + 1)],
+                        lhsT=wdq_codes[:, stationary].bitcast(FP8X4),
+                        lhsT_scale=wdq_scales[:, stationary],
+                        rhs=x_codes[:, moving].bitcast(FP8X4),
+                        rhs_scale=x_scales[:, moving],
+                        start=(g == 0),
+                        stop=(g == 1),
+                    )
+            nc.vector.tensor_copy(
+                out=cq_grouped[:].rearrange("q (r t) -> q r t", t=PACK), in_=bank[:].rearrange("q (t r) -> q r t", t=PACK)
+            )
 
         def times_cq(codes, scales, j):
             bank = psum.tile([P, BANK], F32, tag="bank")
@@ -210,8 +194,7 @@ def tile_causalselfattention_pa_s_kernel(tc, x, cos, sin, W_dq, W_uq, W_uk, W_qr
                 out=out_0[0, 4 * j : 4 * j + 4].rearrange("h r n -> r h n"), in_=q_abs[:].rearrange("r (h n) -> r h n", n=P)
             )
 
-        def rotated(j):
-            bank = times_cq(wqr_codes, wqr_scales, j)
+        def rotate(j, bank):
             half = BANK // 2
             by_cos = keep.tile([P, BANK], F32, name="by_cos%d" % j)
             by_sin = keep.tile([P, BANK], F32, name="by_sin%d" % j)
@@ -242,7 +225,35 @@ def tile_causalselfattention_pa_s_kernel(tc, x, cos, sin, W_dq, W_uq, W_uk, W_qr
             )
             nc.sync.dma_start(out=out_1[0, :, 4 * j : 4 * j + 4, :].rearrange("r h d -> r (h d)"), in_=q_r[:])
 
-        rotated(0)
+        transpose_words(0, x_sb[:], x_grouped[:].bitcast(F32))
+        transpose_a(0, 0)
+        quantise(x_codes, x_scales, x_grouped, 0, 2 * P)
+        transpose_a(1, 1)
+        for s in range(PACK):
+            transpose_wdq(s)
+            if s >= 1:
+                quantise(wdq_codes, wdq_scales, wdq_grouped, 2 * P * (s - 1), 2 * P)
+        quantise(wdq_codes, wdq_scales, wdq_grouped, 2 * P * (PACK - 1), 2 * P)
+        for h in range(4):
+            multiply_keff(h, h)
+        quantise_keff(0)
+        transpose_wqr(0)
+        transpose_wqr(1)
+        quantise_keff(1)
+        latent()
+        quantise(wqr_codes, wqr_scales, wqr_grouped, 0, BANK)
+        quantise(cq_codes, cq_scales, cq_grouped, 0, P)
+        transpose_a(2, SCALAR)
+        transpose_a(3, SCALAR)
+        transpose_wqr(2)
+        transpose_wqr(3)
+        rotate(0, times_cq(wqr_codes, wqr_scales, 0))
+        for h in range(4, HEADS):
+            multiply_keff(h, SCALAR)
+        quantise(wqr_codes, wqr_scales, wqr_grouped, BANK, BANK)
+        c_qr1 = times_cq(wqr_codes, wqr_scales, 1)
         absorbed(0)
+        quantise_keff(2)
+        quantise_keff(3)
+        rotate(1, c_qr1)
         absorbed(1)
-        rotated(1)

@@ -57,10 +57,10 @@ def tile_causalselfattention_pa_s_kernel(tc, x, cos, sin, W_dq, W_uq, W_uk, W_qr
             nc.sync.dma_start(out=wdq_sb[:, v].rearrange("q e c -> q (e c)"), in_=wdq_dram[:, v])
         nc.sync.dma_start(out=u_sb[:], in_=W_uk.rearrange("(h d) n -> d h n", h=HEADS))
         load_wqr(0)
+        nc.sync.dma_start(out=cos_sb[:], in_=cos)
+        nc.sync.dma_start(out=sin_sb[:], in_=sin)
         load_a(4)
         load_wqr(1)
-        nc.scalar.dma_start(out=cos_sb[:], in_=cos)
-        nc.scalar.dma_start(out=sin_sb[:], in_=sin)
 
         ident_f32 = keep.tile([P, P], F32)
         make_identity(nc, ident_f32[:])
@@ -194,11 +194,11 @@ def tile_causalselfattention_pa_s_kernel(tc, x, cos, sin, W_dq, W_uq, W_uk, W_qr
                 out=out_0[0, 4 * j : 4 * j + 4].rearrange("h r n -> r h n"), in_=q_abs[:].rearrange("r (h n) -> r h n", n=P)
             )
 
-        def rotate(j, bank):
+        def rotation_products(j):
+            bank = times_cq(wqr_codes, wqr_scales, j)
             half = BANK // 2
             by_cos = keep.tile([P, BANK], F32, name="by_cos%d" % j)
             by_sin = keep.tile([P, BANK], F32, name="by_sin%d" % j)
-            q_r = keep.tile([P, BANK], F32, name="q_r%d" % j)
             nc.vector.tensor_tensor(
                 out=by_cos[:].rearrange("r (k i) -> r k i", i=HALF),
                 in0=bank[:].rearrange("r (k i) -> r k i", i=HALF),
@@ -217,6 +217,10 @@ def tile_causalselfattention_pa_s_kernel(tc, x, cos, sin, W_dq, W_uq, W_uk, W_qr
                 in1=sin_sb[:].unsqueeze(1).to_broadcast([P, half // HALF, HALF]),
                 op=MULT,
             )
+            return by_cos, by_sin
+
+        def rotation_sum(j, by_cos, by_sin):
+            q_r = keep.tile([P, BANK], F32, name="q_r%d" % j)
             nc.vector.tensor_tensor(
                 out=q_r[:].rearrange("r (c e) -> r c e", e=2),
                 in0=by_cos[:].rearrange("r (e c) -> r c e", e=2),
@@ -229,11 +233,11 @@ def tile_causalselfattention_pa_s_kernel(tc, x, cos, sin, W_dq, W_uq, W_uk, W_qr
         transpose_a(0, 0)
         quantise(x_codes, x_scales, x_grouped, 0, 2 * P)
         transpose_a(1, 1)
-        for s in range(PACK):
-            transpose_wdq(s)
-            if s >= 1:
-                quantise(wdq_codes, wdq_scales, wdq_grouped, 2 * P * (s - 1), 2 * P)
-        quantise(wdq_codes, wdq_scales, wdq_grouped, 2 * P * (PACK - 1), 2 * P)
+        for s in range(PACK + 2):
+            if s < PACK:
+                transpose_wdq(s)
+            if s >= 2:
+                quantise(wdq_codes, wdq_scales, wdq_grouped, 2 * P * (s - 2), 2 * P)
         for h in range(4):
             multiply_keff(h, h)
         quantise_keff(0)
@@ -247,13 +251,14 @@ def tile_causalselfattention_pa_s_kernel(tc, x, cos, sin, W_dq, W_uq, W_uk, W_qr
         transpose_a(3, SCALAR)
         transpose_wqr(2)
         transpose_wqr(3)
-        rotate(0, times_cq(wqr_codes, wqr_scales, 0))
+        products = rotation_products(0)
+        quantise(wqr_codes, wqr_scales, wqr_grouped, BANK, BANK)
+        rotation_sum(0, *products)
         for h in range(4, HEADS):
             multiply_keff(h, SCALAR)
-        quantise(wqr_codes, wqr_scales, wqr_grouped, BANK, BANK)
-        c_qr1 = times_cq(wqr_codes, wqr_scales, 1)
-        absorbed(0)
         quantise_keff(2)
+        products = rotation_products(1)
+        absorbed(0)
         quantise_keff(3)
-        rotate(1, c_qr1)
+        rotation_sum(1, *products)
         absorbed(1)

@@ -138,14 +138,13 @@ def tile_causalselfattention_pa_s_kernel(tc, x, cos, sin, W_dq, W_uq, W_uk, W_qr
                 )
             empty(number, out=at_sb[:, 2 * pair : 2 * pair + 2].rearrange("d h t q -> d (h t q)"), in_=bank[:])
 
-        def multiply_keff(h, number):
+        def multiply_keff(h):
             bank = psum.tile([P, BANK], F32, tag="bank")
             for t in range(PACK):
                 nc.tensor.matmul(
                     out=bank[:, P * t : P * (t + 1)], lhsT=at_sb[:, h, t, :], rhs=u_sb[:, h, :], start=True, stop=True
                 )
-            empty(
-                number,
+            nc.scalar.copy(
                 out=keff_grouped[:, BANK * h : BANK * (h + 1)].rearrange("q (n t) -> q n t", t=PACK),
                 in_=bank[:].rearrange("q (t n) -> q n t", t=PACK),
             )
@@ -194,8 +193,7 @@ def tile_causalselfattention_pa_s_kernel(tc, x, cos, sin, W_dq, W_uq, W_uk, W_qr
                 out=out_0[0, 4 * j : 4 * j + 4].rearrange("h r n -> r h n"), in_=q_abs[:].rearrange("r (h n) -> r h n", n=P)
             )
 
-        def rotation_products(j):
-            bank = times_cq(wqr_codes, wqr_scales, j)
+        def rotation_products(j, bank):
             half = BANK // 2
             by_cos = keep.tile([P, BANK], F32, name="by_cos%d" % j)
             by_sin = keep.tile([P, BANK], F32, name="by_sin%d" % j)
@@ -239,26 +237,26 @@ def tile_causalselfattention_pa_s_kernel(tc, x, cos, sin, W_dq, W_uq, W_uk, W_qr
             if s >= 2:
                 quantise(wdq_codes, wdq_scales, wdq_grouped, 2 * P * (s - 2), 2 * P)
         for h in range(4):
-            multiply_keff(h, h)
-        quantise_keff(0)
+            multiply_keff(h)
         transpose_wqr(0)
         transpose_wqr(1)
-        quantise_keff(1)
         latent()
-        quantise(wqr_codes, wqr_scales, wqr_grouped, 0, BANK)
+        quantise_keff(0)
         quantise(cq_codes, cq_scales, cq_grouped, 0, P)
+        quantise(wqr_codes, wqr_scales, wqr_grouped, 0, BANK)
+        quantise_keff(1)
         transpose_a(2, SCALAR)
         transpose_a(3, SCALAR)
         transpose_wqr(2)
         transpose_wqr(3)
-        products = rotation_products(0)
+        products = rotation_products(0, times_cq(wqr_codes, wqr_scales, 0))
         quantise(wqr_codes, wqr_scales, wqr_grouped, BANK, BANK)
         rotation_sum(0, *products)
         for h in range(4, HEADS):
-            multiply_keff(h, SCALAR)
-        quantise_keff(2)
-        products = rotation_products(1)
+            multiply_keff(h)
+        c_qr1 = times_cq(wqr_codes, wqr_scales, 1)
         absorbed(0)
+        quantise_keff(2)
         quantise_keff(3)
-        rotation_sum(1, *products)
         absorbed(1)
+        rotation_sum(1, *rotation_products(1, c_qr1))

@@ -18,6 +18,7 @@ C = 1024
 L = 512
 HEADS = 8
 HALF = 64
+WARM_UP = 4
 
 FLOPS = 2 * P * C * L + 2 * HEADS * L * P * P + 2 * HEADS * P * L * P + 2 * P * L * HEADS * P
 
@@ -66,6 +67,11 @@ def tile_causalselfattention_pa_s_kernel(tc, x, cos, sin, W_dq, W_uq, W_uk, W_qr
         make_identity(nc, ident_f32[:])
         ident_bf16 = keep.tile([P, P], BF16)
         make_identity(nc, ident_bf16[:])
+        warm = psum.tile([P, BANK], F32, tag="bank")
+        for piece in range(WARM_UP):
+            nc.tensor.matmul(
+                out=warm[:, P * piece : P * (piece + 1)], lhsT=ident_f32[:], rhs=ident_f32[:], start=True, stop=True
+            )
         minus_sin = keep.tile([P, HALF], BF16)
         nc.gpsimd.tensor_scalar_mul(minus_sin[:], sin_sb[:], -1.0)
 

@@ -18,7 +18,7 @@ C = 1024
 L = 512
 HEADS = 8
 HALF = 64
-WARM_UP = 4
+WARM_UP = 6
 
 FLOPS = 2 * P * C * L + 2 * HEADS * L * P * P + 2 * HEADS * P * L * P + 2 * P * L * HEADS * P
 
@@ -63,15 +63,17 @@ def tile_causalselfattention_pa_s_kernel(tc, x, cos, sin, W_dq, W_uq, W_uk, W_qr
         load_a(4)
         load_wqr(1)
 
+        zeros = keep.tile([P, P], F32)
+        nc.vector.memset(zeros[:], 0.0)
+        warm = psum.tile([P, BANK], F32, tag="bank")
+        for number in range(WARM_UP):
+            piece = number % (BANK // P)
+            nc.tensor.matmul(out=warm[:, P * piece : P * (piece + 1)], lhsT=zeros[:], rhs=zeros[:], start=True, stop=True)
+
         ident_f32 = keep.tile([P, P], F32)
         make_identity(nc, ident_f32[:])
         ident_bf16 = keep.tile([P, P], BF16)
         make_identity(nc, ident_bf16[:])
-        warm = psum.tile([P, BANK], F32, tag="bank")
-        for piece in range(WARM_UP):
-            nc.tensor.matmul(
-                out=warm[:, P * piece : P * (piece + 1)], lhsT=ident_f32[:], rhs=ident_f32[:], start=True, stop=True
-            )
         minus_sin = keep.tile([P, HALF], BF16)
         nc.gpsimd.tensor_scalar_mul(minus_sin[:], sin_sb[:], -1.0)
 

@@ -46,6 +46,10 @@ def tile_causalselfattention_pa_s_kernel(tc, x, cos, sin, W_dq, W_uq, W_uk, W_qr
             for v in range(2):
                 nc.sync.dma_start(out=a_sb[:, v, :, columns], in_=a_dram[:, v, :, columns])
 
+        def load_u(first_head):
+            heads = slice(first_head, first_head + 4)
+            nc.sync.dma_start(out=u_sb[:, heads], in_=W_uk.rearrange("(h d) n -> d h n", h=HEADS)[:, heads])
+
         def load_wqr(j):
             nc.sync.dma_start(
                 out=wqr_sb[:, 2 * j : 2 * j + 2].rearrange("q b e l -> q b (e l)"),
@@ -56,12 +60,13 @@ def tile_causalselfattention_pa_s_kernel(tc, x, cos, sin, W_dq, W_uq, W_uk, W_qr
         load_a(0)
         for v in range(2):
             nc.sync.dma_start(out=wdq_sb[:, v].rearrange("q e c -> q (e c)"), in_=wdq_dram[:, v])
-        nc.sync.dma_start(out=u_sb[:], in_=W_uk.rearrange("(h d) n -> d h n", h=HEADS))
+        load_u(0)
         load_wqr(0)
-        nc.sync.dma_start(out=cos_sb[:], in_=cos)
-        nc.sync.dma_start(out=sin_sb[:], in_=sin)
         load_a(4)
         load_wqr(1)
+        load_u(4)
+        nc.sync.dma_start(out=cos_sb[:], in_=cos)
+        nc.sync.dma_start(out=sin_sb[:], in_=sin)
 
         zeros = keep.tile([P, P], F32)
         nc.vector.memset(zeros[:], 0.0)

@@ -206,7 +206,7 @@ def tile_causalselfattention_pa_s_kernel(tc, x, cos, sin, W_dq, W_uq, W_uk, W_qr
                 out=out_0[0, 4 * j : 4 * j + 4].rearrange("h r n -> r h n"), in_=q_abs[:].rearrange("r (h n) -> r h n", n=P)
             )
 
-        def rotation_products(j, bank):
+        def rotation_products(j, bank, pieces):
             half = BANK // 2
             by_cos = keep.tile([P, BANK], F32, name="by_cos%d" % j)
             by_sin = keep.tile([P, BANK], F32, name="by_sin%d" % j)
@@ -222,23 +222,35 @@ def tile_causalselfattention_pa_s_kernel(tc, x, cos, sin, W_dq, W_uq, W_uk, W_qr
                 in1=minus_sin[:].unsqueeze(1).to_broadcast([P, half // HALF, HALF]),
                 op=MULT,
             )
-            nc.vector.tensor_tensor(
-                out=by_sin[:, half:BANK].rearrange("r (k i) -> r k i", i=HALF),
-                in0=bank[:, 0:half].rearrange("r (k i) -> r k i", i=HALF),
-                in1=sin_sb[:].unsqueeze(1).to_broadcast([P, half // HALF, HALF]),
-                op=MULT,
-            )
+            width = half // pieces
+            for piece in range(pieces):
+                nc.vector.tensor_tensor(
+                    out=by_sin[:, half + width * piece : half + width * (piece + 1)].rearrange("r (k i) -> r k i", i=HALF),
+                    in0=bank[:, width * piece : width * (piece + 1)].rearrange("r (k i) -> r k i", i=HALF),
+                    in1=sin_sb[:].unsqueeze(1).to_broadcast([P, width // HALF, HALF]),
+                    op=MULT,
+                )
             return by_cos, by_sin
 
-        def rotation_sum(j, by_cos, by_sin):
+        def rotation_sum(j, by_cos, by_sin, pieces):
             q_r = keep.tile([P, BANK], F32, name="q_r%d" % j)
-            nc.vector.tensor_tensor(
-                out=q_r[:].rearrange("r (c e) -> r c e", e=2),
-                in0=by_cos[:].rearrange("r (e c) -> r c e", e=2),
-                in1=by_sin[:].rearrange("r (e c) -> r c e", e=2),
-                op=ADD,
-            )
-            nc.sync.dma_start(out=out_1[0, :, 4 * j : 4 * j + 4, :].rearrange("r h d -> r (h d)"), in_=q_r[:])
+            width = BANK // 2 // pieces
+            heads = 4 // pieces
+            for piece in range(pieces):
+                pairs = slice(width * piece, width * (piece + 1))
+                columns = slice(2 * width * piece, 2 * width * (piece + 1))
+                nc.vector.tensor_tensor(
+                    out=q_r[:, columns].rearrange("r (c e) -> r c e", e=2),
+                    in0=by_cos[:].rearrange("r (e c) -> r c e", e=2)[:, pairs, :],
+                    in1=by_sin[:].rearrange("r (e c) -> r c e", e=2)[:, pairs, :],
+                    op=ADD,
+                )
+            for piece in range(pieces):
+                first_head = 4 * j + heads * piece
+                nc.sync.dma_start(
+                    out=out_1[0, :, first_head : first_head + heads, :].rearrange("r h d -> r (h d)"),
+                    in_=q_r[:, 2 * width * piece : 2 * width * (piece + 1)],
+                )
 
         transpose_words(0, x_sb[:], x_grouped[:].bitcast(F32))
         transpose_a(0, 0)
@@ -262,9 +274,9 @@ def tile_causalselfattention_pa_s_kernel(tc, x, cos, sin, W_dq, W_uq, W_uk, W_qr
         transpose_a(3, SCALAR)
         transpose_wqr(2)
         transpose_wqr(3)
-        products = rotation_products(0, times_cq(wqr_codes, wqr_scales, 0))
+        products = rotation_products(0, times_cq(wqr_codes, wqr_scales, 0), 1)
         quantise(wqr_codes, wqr_scales, wqr_grouped, BANK, BANK)
-        rotation_sum(0, *products)
+        rotation_sum(0, *products, 1)
         for h in range(4, HEADS):
             multiply_keff(h)
         c_qr1 = times_cq(wqr_codes, wqr_scales, 1)
@@ -272,4 +284,4 @@ def tile_causalselfattention_pa_s_kernel(tc, x, cos, sin, W_dq, W_uq, W_uk, W_qr
         quantise_keff(2)
         quantise_keff(3)
         absorbed(1)
-        rotation_sum(1, *rotation_products(1, c_qr1))
+        rotation_sum(1, *rotation_products(1, c_qr1, 2), 2)

@@ -184,11 +184,11 @@ def tile_causalselfattention_pa_s_kernel(tc, x, cos, sin, W_dq, W_uq, W_uk, W_qr
                 out=cq_grouped[:].rearrange("q (r t) -> q r t", t=PACK), in_=bank[:].rearrange("q (t r) -> q r t", t=PACK)
             )
 
-        def times_cq(codes, scales, j):
+        def times_cq(codes, scales, first_column, width):
             bank = psum.tile([P, BANK], F32, tag="bank")
-            columns = slice(BANK * j, BANK * (j + 1))
+            columns = slice(first_column, first_column + width)
             nc.tensor.matmul_mx(
-                out=bank[:],
+                out=bank[:, 0:width],
                 lhsT=cq_codes[:].bitcast(FP8X4),
                 lhsT_scale=cq_scales[:],
                 rhs=codes[:, columns].bitcast(FP8X4),
@@ -198,12 +198,14 @@ def tile_causalselfattention_pa_s_kernel(tc, x, cos, sin, W_dq, W_uq, W_uk, W_qr
             )
             return bank
 
-        def absorbed(j):
-            bank = times_cq(keff_codes, keff_scales, j)
-            q_abs = keep.tile([P, BANK], F32, name="q_abs%d" % j)
-            nc.scalar.copy(out=q_abs[:], in_=bank[:])
+        def absorbed(first_head, heads):
+            width = P * heads
+            bank = times_cq(keff_codes, keff_scales, P * first_head, width)
+            q_abs = keep.tile([P, width], F32, name="q_abs%d" % first_head)
+            nc.scalar.copy(out=q_abs[:], in_=bank[:, 0:width])
             nc.sync.dma_start(
-                out=out_0[0, 4 * j : 4 * j + 4].rearrange("h r n -> r h n"), in_=q_abs[:].rearrange("r (h n) -> r h n", n=P)
+                out=out_0[0, first_head : first_head + heads].rearrange("h r n -> r h n"),
+                in_=q_abs[:].rearrange("r (h n) -> r h n", n=P),
             )
 
         def rotation_products(j, bank, pieces):
@@ -274,14 +276,15 @@ def tile_causalselfattention_pa_s_kernel(tc, x, cos, sin, W_dq, W_uq, W_uk, W_qr
         transpose_a(3, SCALAR)
         transpose_wqr(2)
         transpose_wqr(3)
-        products = rotation_products(0, times_cq(wqr_codes, wqr_scales, 0), 1)
+        products = rotation_products(0, times_cq(wqr_codes, wqr_scales, 0, BANK), 1)
         quantise(wqr_codes, wqr_scales, wqr_grouped, BANK, BANK)
         rotation_sum(0, *products, 1)
         for h in range(4, HEADS):
             multiply_keff(h)
-        c_qr1 = times_cq(wqr_codes, wqr_scales, 1)
-        absorbed(0)
+        c_qr1 = times_cq(wqr_codes, wqr_scales, BANK, BANK)
+        absorbed(0, 4)
         quantise_keff(2)
+        absorbed(4, 2)
         quantise_keff(3)
-        absorbed(1)
+        absorbed(6, 2)
         rotation_sum(1, *rotation_products(1, c_qr1, 2), 2)

from contextlib import ExitStack

import concourse.mybir as mybir
from concourse.masks import make_identity

F32 = mybir.dt.float32
BF16 = mybir.dt.bfloat16
U32 = mybir.dt.uint32
U8 = mybir.dt.uint8
FP8X4 = mybir.dt.float8_e4m3fn_x4
MULT = mybir.AluOpType.mult
ADD = mybir.AluOpType.add

P = 128
PACK = 4
BANK = 512
C = 1024
L = 512
HEADS = 8
HALF = 64
WARM_UP = 6

FLOPS = 2 * P * C * L + 2 * HEADS * L * P * P + 2 * HEADS * P * L * P + 2 * P * L * HEADS * P


def tile_causalselfattention_pa_s_kernel(tc, x, cos, sin, W_dq, W_uq, W_uk, W_qr, out_0, out_1):
    nc = tc.nc
    with ExitStack() as ctx:
        keep = ctx.enter_context(tc.tile_pool(name="keep", bufs=1))
        psum = ctx.enter_context(tc.psum_pool(name="psum", bufs=8))
        ctx.enter_context(tc.manual_schedule())

        a_sb = keep.tile([P, 2, 2, C], BF16)
        a_dram = W_uq.rearrange("(v q e two) c -> q v e (two c)", v=2, e=2, two=2)
        u_sb = keep.tile([P, HEADS, P], BF16)
        x_sb = keep.tile([P, C], BF16)
        wdq_sb = keep.tile([P, 2, 2, C], BF16)
        wdq_dram = W_dq.rearrange("(v q e) c -> q v (e c)", v=2, e=2)
        wqr_sb = keep.tile([P, 4, 2, L], BF16)
        wqr_dram = W_qr.rearrange("(b q e) l -> q b (e l)", b=4, e=2)
        cos_sb = keep.tile([P, HALF], BF16)
        sin_sb = keep.tile([P, HALF], BF16)

        def load_a(first_head):
            columns = slice(P * first_head, P * (first_head + 4))
            for v in range(2):
                nc.sync.dma_start(out=a_sb[:, v, :, columns], in_=a_dram[:, v, :, columns])

        def load_u(first_head):
            heads = slice(first_head, first_head + 4)
            nc.sync.dma_start(out=u_sb[:, heads], in_=W_uk.rearrange("(h d) n -> d h n", h=HEADS)[:, heads])

        def load_wqr(j):
            nc.sync.dma_start(
                out=wqr_sb[:, 2 * j : 2 * j + 2].rearrange("q b e l -> q b (e l)"),
                in_=wqr_dram[:, 2 * j : 2 * j + 2],
            )

        nc.sync.dma_start(out=x_sb[:], in_=x[0])
        load_a(0)
        for v in range(2):
            nc.sync.dma_start(out=wdq_sb[:, v].rearrange("q e c -> q (e c)"), in_=wdq_dram[:, v])
        load_u(0)
        load_wqr(0)
        load_a(4)
        load_wqr(1)
        load_u(4)
        nc.sync.dma_start(out=cos_sb[:], in_=cos)
        nc.sync.dma_start(out=sin_sb[:], in_=sin)

        zeros = keep.tile([P, P], F32)
        nc.vector.memset(zeros[:], 0.0)
        warm = psum.tile([P, BANK], F32, tag="bank")
        for number in range(WARM_UP):
            piece = number % (BANK // P)
            nc.tensor.matmul(out=warm[:, P * piece : P * (piece + 1)], lhsT=zeros[:], rhs=zeros[:], start=True, stop=True)

        ident_f32 = keep.tile([P, P], F32)
        make_identity(nc, ident_f32[:])
        ident_bf16 = keep.tile([P, P], BF16)
        make_identity(nc, ident_bf16[:])
        minus_sin = keep.tile([P, HALF], BF16)
        nc.gpsimd.tensor_scalar_mul(minus_sin[:], sin_sb[:], -1.0)

        at_sb = keep.tile([P, HEADS, PACK, P], BF16)
        keff_grouped = keep.tile([P, HEADS * P * PACK], BF16, align_bytes=64)
        keff_codes = keep.tile([P, HEADS * P], U32, align_bytes=64)
        keff_scales = keep.tile([P, HEADS * P], U8, align_bytes=64)
        x_grouped = keep.tile([P, 2 * P * PACK], BF16, align_bytes=64)
        x_codes = keep.tile([P, 2 * P], U32, align_bytes=64)
        x_scales = keep.tile([P, 2 * P], U8, align_bytes=64)
        wdq_grouped = keep.tile([P, PACK * 2 * P * PACK], BF16, align_bytes=64)
        wdq_codes = keep.tile([P, PACK * 2 * P], U32, align_bytes=64)
        wdq_scales = keep.tile([P, PACK * 2 * P], U8, align_bytes=64)
        cq_grouped = keep.tile([P, P * PACK], BF16, align_bytes=64)
        cq_codes = keep.tile([P, P], U32, align_bytes=64)
        cq_scales = keep.tile([P, P], U8, align_bytes=64)
        wqr_grouped = keep.tile([P, HEADS * P * PACK], BF16, align_bytes=64)
        wqr_codes = keep.tile([P, HEADS * P], U32, align_bytes=64)
        wqr_scales = keep.tile([P, HEADS * P], U8, align_bytes=64)

        def quantise(codes, scales, grouped, first_word, words):
            nc.vector.quantize_mx(
                out=codes[:, first_word : first_word + words].bitcast(FP8X4),
                scales=scales[:, first_word : first_word + words],
                in_=grouped[:, PACK * first_word : PACK * (first_word + words)],
            )

        def empty(number, out, in_):
            if number % 2 == 0:
                nc.vector.tensor_copy(out=out, in_=in_)
            else:
                nc.scalar.copy(out=out, in_=in_)

        SCALAR = 1

        def transpose_words(number, rows, grouped_words):
            words = rows.bitcast(F32)
            bank = psum.tile([P, BANK], F32, tag="bank")
            for piece in range(BANK // P):
                nc.tensor.transpose(
                    bank[:, P * piece : P * (piece + 1)], words[:, P * piece : P * (piece + 1)], ident_f32[:]
                )
            empty(
                number,
                out=grouped_words.rearrange("q (g r v) -> q g r v", r=P, v=2),
                in_=bank[:].rearrange("q (g v r) -> q g r v", r=P, v=2),
            )

        def transpose_wdq(s):
            transpose_words(s, wdq_sb[:, s // 2, s % 2, :], wdq_grouped[:, 2 * BANK * s : 2 * BANK * (s + 1)].bitcast(F32))

        def transpose_wqr(b):
            bank = psum.tile([P, BANK], F32, tag="bank")
            for piece in range(BANK // P):
                e, v = piece // 2, piece % 2
                nc.tensor.transpose(
                    bank[:, P * piece : P * (piece + 1)],
                    wqr_sb[:, b, e, :].bitcast(F32)[:, P * v : P * (v + 1)],
                    ident_f32[:],
                )
            grouped_words = wqr_grouped[:].bitcast(F32).rearrange("q (j e b r v) -> q j e b r v", j=2, e=2, b=2, v=2)
            empty(b, out=grouped_words[:, b // 2, :, b % 2, :, :], in_=bank[:].rearrange("q (e v r) -> q e r v", e=2, v=2))

        def transpose_a(pair, number):
            bank = psum.tile([P, 2 * PACK * P], BF16, tag="bank")
            for piece in range(2 * PACK):
                h, t = 2 * pair + piece // PACK, piece % PACK
                nc.tensor.transpose(
                    bank[:, P * piece : P * (piece + 1)], a_sb[:, t // 2, t % 2, P * h : P * (h + 1)], ident_bf16[:]
                )
            empty(number, out=at_sb[:, 2 * pair : 2 * pair + 2].rearrange("d h t q -> d (h t q)"), in_=bank[:])

        def multiply_keff(h):
            bank = psum.tile([P, BANK], F32, tag="bank")
            for t in range(PACK):
                nc.tensor.matmul(
                    out=bank[:, P * t : P * (t + 1)], lhsT=at_sb[:, h, t, :], rhs=u_sb[:, h, :], start=True, stop=True
                )
            nc.scalar.copy(
                out=keff_grouped[:, BANK * h : BANK * (h + 1)].rearrange("q (n t) -> q n t", t=PACK),
                in_=bank[:].rearrange("q (t n) -> q n t", t=PACK),
            )

        def quantise_keff(pair):
            quantise(keff_codes, keff_scales, keff_grouped, 2 * P * pair, 2 * P)

        def latent():
            bank = psum.tile([P, BANK], F32, tag="bank")
            for s in range(PACK):
                for g in range(2):
                    stationary = slice(2 * P * s + P * g, 2 * P * s + P * (g + 1))
                    moving = slice(P * g, P * (g + 1))
                    nc.tensor.matmul_mx(
                        out=bank[:, P * s : P * (s + 1)],
                        lhsT=wdq_codes[:, stationary].bitcast(FP8X4),
                        lhsT_scale=wdq_scales[:, stationary],
                        rhs=x_codes[:, moving].bitcast(FP8X4),
                        rhs_scale=x_scales[:, moving],
                        start=(g == 0),
                        stop=(g == 1),
                    )
            nc.vector.tensor_copy(
                out=cq_grouped[:].rearrange("q (r t) -> q r t", t=PACK), in_=bank[:].rearrange("q (t r) -> q r t", t=PACK)
            )

        def times_cq(codes, scales, first_column, width):
            bank = psum.tile([P, BANK], F32, tag="bank")
            columns = slice(first_column, first_column + width)
            nc.tensor.matmul_mx(
                out=bank[:, 0:width],
                lhsT=cq_codes[:].bitcast(FP8X4),
                lhsT_scale=cq_scales[:],
                rhs=codes[:, columns].bitcast(FP8X4),
                rhs_scale=scales[:, columns],
                start=True,
                stop=True,
            )
            return bank

        def absorbed(first_head, heads):
            width = P * heads
            bank = times_cq(keff_codes, keff_scales, P * first_head, width)
            q_abs = keep.tile([P, width], F32, name="q_abs%d" % first_head)
            nc.scalar.copy(out=q_abs[:], in_=bank[:, 0:width])
            nc.sync.dma_start(
                out=out_0[0, first_head : first_head + heads].rearrange("h r n -> r h n"),
                in_=q_abs[:].rearrange("r (h n) -> r h n", n=P),
            )

        def rotation_products(j, bank, pieces):
            half = BANK // 2
            by_cos = keep.tile([P, BANK], F32, name="by_cos%d" % j)
            by_sin = keep.tile([P, BANK], F32, name="by_sin%d" % j)
            nc.vector.tensor_tensor(
                out=by_cos[:].rearrange("r (k i) -> r k i", i=HALF),
                in0=bank[:].rearrange("r (k i) -> r k i", i=HALF),
                in1=cos_sb[:].unsqueeze(1).to_broadcast([P, BANK // HALF, HALF]),
                op=MULT,
            )
            nc.vector.tensor_tensor(
                out=by_sin[:, 0:half].rearrange("r (k i) -> r k i", i=HALF),
                in0=bank[:, half:BANK].rearrange("r (k i) -> r k i", i=HALF),
                in1=minus_sin[:].unsqueeze(1).to_broadcast([P, half // HALF, HALF]),
                op=MULT,
            )
            width = half // pieces
            for piece in range(pieces):
                nc.vector.tensor_tensor(
                    out=by_sin[:, half + width * piece : half + width * (piece + 1)].rearrange("r (k i) -> r k i", i=HALF),
                    in0=bank[:, width * piece : width * (piece + 1)].rearrange("r (k i) -> r k i", i=HALF),
                    in1=sin_sb[:].unsqueeze(1).to_broadcast([P, width // HALF, HALF]),
                    op=MULT,
                )
            return by_cos, by_sin

        def rotation_sum(j, by_cos, by_sin, pieces):
            q_r = keep.tile([P, BANK], F32, name="q_r%d" % j)
            width = BANK // 2 // pieces
            heads = 4 // pieces
            for piece in range(pieces):
                pairs = slice(width * piece, width * (piece + 1))
                columns = slice(2 * width * piece, 2 * width * (piece + 1))
                nc.vector.tensor_tensor(
                    out=q_r[:, columns].rearrange("r (c e) -> r c e", e=2),
                    in0=by_cos[:].rearrange("r (e c) -> r c e", e=2)[:, pairs, :],
                    in1=by_sin[:].rearrange("r (e c) -> r c e", e=2)[:, pairs, :],
                    op=ADD,
                )
            for piece in range(pieces):
                first_head = 4 * j + heads * piece
                nc.sync.dma_start(
                    out=out_1[0, :, first_head : first_head + heads, :].rearrange("r h d -> r (h d)"),
                    in_=q_r[:, 2 * width * piece : 2 * width * (piece + 1)],
                )

        transpose_words(0, x_sb[:], x_grouped[:].bitcast(F32))
        transpose_a(0, 0)
        quantise(x_codes, x_scales, x_grouped, 0, 2 * P)
        transpose_a(1, 1)
        for s in range(PACK + 2):
            if s < PACK:
                transpose_wdq(s)
            if s >= 2:
                quantise(wdq_codes, wdq_scales, wdq_grouped, 2 * P * (s - 2), 2 * P)
        for h in range(4):
            multiply_keff(h)
        transpose_wqr(0)
        transpose_wqr(1)
        latent()
        quantise_keff(0)
        quantise(cq_codes, cq_scales, cq_grouped, 0, P)
        quantise(wqr_codes, wqr_scales, wqr_grouped, 0, BANK)
        quantise_keff(1)
        transpose_a(2, SCALAR)
        transpose_a(3, SCALAR)
        transpose_wqr(2)
        transpose_wqr(3)
        products = rotation_products(0, times_cq(wqr_codes, wqr_scales, 0, BANK), 1)
        quantise(wqr_codes, wqr_scales, wqr_grouped, BANK, BANK)
        rotation_sum(0, *products, 1)
        for h in range(4, HEADS):
            multiply_keff(h)
        c_qr1 = times_cq(wqr_codes, wqr_scales, BANK, BANK)
        absorbed(0, 4)
        quantise_keff(2)
        absorbed(4, 2)
        quantise_keff(3)
        absorbed(6, 2)
        rotation_sum(1, *rotation_products(1, c_qr1, 2), 2)
